import numpy as np
import ml_dtypes


def mxq(x, axis, fmt="e4m3"):
    dtype, down = {"e4m3": (ml_dtypes.float8_e4m3fn, 7), "e5m2": (ml_dtypes.float8_e5m2, 14)}[fmt]
    v = np.moveaxis(np.asarray(x, np.float32).astype(ml_dtypes.bfloat16).astype(np.float64), axis, -1)
    blocks = v.reshape(v.shape[:-1] + (-1, 32))
    amax = np.abs(blocks).max(-1, keepdims=True)
    byte = np.maximum(np.where(amax > 0, np.frexp(amax)[1] - 1 + 127, 0) - down, 1)
    scale = np.exp2(byte - 127.0)
    codes = (blocks / scale).astype(np.float32).astype(dtype).astype(np.float64)
    return np.moveaxis((codes * scale).reshape(v.shape), -1, axis)


WIDE = False


def mx_kscale(k):
    if not WIDE:
        return np.ones(k)
    levels = np.array([10, -10, 5, -5, 0])
    a = np.random.permutation(np.resize(levels, k // 512 * 4)).reshape(k // 512, 4)
    idx = np.arange(k)
    return np.exp2(a[idx // 512, idx % 128 // 32])


BF16 = ml_dtypes.bfloat16


def bf(x):
    return np.asarray(x, np.float32).astype(BF16)


def f64(x):
    return np.asarray(x).astype(np.float64)


B, N, D = 4, 256, 512
BN = B * N
DM = D + D


def sigmoid(v):
    return 1.0 / (1.0 + np.exp(-v))


def setup_inputs():
    s = mx_kscale(DM)
    return {"node_state": bf(np.random.standard_normal((B, N, D))),
            "message": bf(np.random.standard_normal((B, N, DM)) * s),
            "h_tilda": bf(np.tanh(np.random.standard_normal((BN, D)))),
            "mask": bf(np.random.uniform(size=(B, N)) < 0.9),
            "w_z": bf(np.random.standard_normal((DM, D)) / np.sqrt(DM) / s[:, None]),
            "u_z": bf(np.random.standard_normal((D, D)) / np.sqrt(D))}


def reference(node_state, message, h_tilda, mask, w_z, u_z):
    h = f64(node_state).reshape(BN, D)
    m = f64(message).reshape(BN, DM)
    z_t = sigmoid((mxq(m, 1, "e4m3") @ mxq(f64(w_z), 0, "e4m3")) + (mxq(h, 1, "e4m3") @ mxq(f64(u_z), 0, "e4m3")))
    h_t = (1.0 - z_t) * h + z_t * f64(h_tilda)
    h_t = h_t * f64(mask).reshape(BN)[:, None]
    return h_t.reshape(B, N, D)

@@ -1,0 +1,183 @@
+from contextlib import ExitStack
+
+import concourse.mybir as mybir
+from concourse.masks import make_identity
+
+F32 = mybir.dt.float32
+BF16 = mybir.dt.bfloat16
+U32 = mybir.dt.uint32
+U8 = mybir.dt.uint8
+FP8X4 = mybir.dt.float8_e4m3fn_x4
+ALU = mybir.AluOpType
+SIGMOID = mybir.ActivationFunctionType.Sigmoid
+
+P = 128
+PACK = 4
+K_PASS = P * PACK
+ROWS = 1024
+D = 512
+DM = 1024
+K = DM + D
+PASSES = K // K_PASS
+ROW_TILES = ROWS // P
+CHUNK = 2
+CHUNKS = ROW_TILES // CHUNK
+HALVES = 2
+VECTOR_COLS = D // 2
+
+FLOPS = 2 * ROWS * K * D
+
+
+def tile_updatefunction_pb_kernel(tc, node_state, message, h_tilda, mask, w_z, u_z, out):
+    nc = tc.nc
+
+    h_rows = node_state.flatten_outer_dims().rearrange("(p i) d -> p i d", i=ROW_TILES)
+    m_rows = message.flatten_outer_dims().rearrange("(p i) d -> p i d", i=ROW_TILES)
+    cand_rows = h_tilda.rearrange("(p i) d -> p i d", i=ROW_TILES)
+    mask_rows = mask.rearrange("b (q i) -> (b q) i", i=ROW_TILES)
+    out_rows = out.flatten_outer_dims().rearrange("(p i) d -> p i d", i=ROW_TILES)
+
+    with ExitStack() as ctx:
+        const = ctx.enter_context(tc.tile_pool(name="const", bufs=1))
+        weights = ctx.enter_context(tc.tile_pool(name="weights", bufs=1))
+        work = ctx.enter_context(tc.tile_pool(name="work", bufs=CHUNKS))
+        psum_t = ctx.enter_context(tc.psum_pool(name="psum_t", bufs=3))
+        psum_acc = ctx.enter_context(tc.psum_pool(name="psum_acc", bufs=3))
+        psum_diff = ctx.enter_context(tc.psum_pool(name="psum_diff", bufs=2))
+
+        mask_bf = const.tile([P, ROW_TILES], BF16)
+        nc.scalar.dma_start(out=mask_bf[:], in_=mask_rows)
+        zero = const.tile([P, 1], F32)
+        nc.vector.memset(zero[:], 0.0)
+        warm = const.tile([P, 1], F32)
+        nc.scalar.activation(out=warm[:], in_=zero[:], func=SIGMOID)
+        ident = const.tile([P, P], F32)
+        make_identity(nc, ident[:])
+        plus_one = const.tile([P, P], BF16)
+        nc.vector.tensor_copy(out=plus_one[:], in_=ident[:])
+        minus_one = const.tile([P, P], BF16)
+        nc.vector.tensor_scalar_mul(out=minus_one[:], in0=ident[:], scalar1=-1.0)
+        mask_f32 = const.tile([P, ROW_TILES], F32)
+        nc.vector.tensor_copy(out=mask_f32[:], in_=mask_bf[:])
+
+        w_raw = weights.tile([P, PASSES, PACK, D], BF16)
+        for g in range(PASSES):
+            w_pass = w_z[g * K_PASS : (g + 1) * K_PASS, :] if g < DM // K_PASS else u_z
+            nc.sync.dma_start(
+                out=w_raw[:, g].rearrange("p (u e) n -> p u (e n)", u=HALVES),
+                in_=w_pass.rearrange("(u p e) n -> p u (e n)", u=HALVES, p=P),
+            )
+        x_sb = []
+        cand = []
+        for c in range(CHUNKS):
+            tiles = slice(c * CHUNK, (c + 1) * CHUNK)
+            x_c = work.tile([P, CHUNK, K], BF16, name="x_sb")
+            nc.sync.dma_start(out=x_c[:, :, 0:DM], in_=m_rows[:, tiles, :])
+            nc.sync.dma_start(out=x_c[:, :, DM:K], in_=h_rows[:, tiles, :])
+            cand_c = work.tile([P, CHUNK, D], BF16, name="cand")
+            nc.sync.dma_start(out=cand_c[:], in_=cand_rows[:, tiles, :])
+            x_sb.append(x_c)
+            cand.append(cand_c)
+
+        w_grouped = weights.tile([P, PASSES, D, PACK], BF16, align_bytes=64)
+        w_codes = weights.tile([P, PASSES, D], U32, align_bytes=64)
+        w_scales = weights.tile([P, PASSES, D], U8, align_bytes=64)
+
+        def regroup_w(copy, g, cols):
+            copy(
+                out=w_grouped[:, g, cols, :].rearrange("p (c i) t -> p c t i", i=4),
+                in_=w_raw[:, g, :, cols].rearrange("p t (c i) -> p c t i", i=4),
+            )
+
+        for g in range(PASSES):
+            regroup_w(nc.vector.tensor_copy, g, slice(0, VECTOR_COLS))
+            regroup_w(nc.scalar.copy, g, slice(VECTOR_COLS, D))
+        for g in range(PASSES):
+            nc.vector.quantize_mx(
+                out=w_codes[:, g, :].bitcast(FP8X4),
+                scales=w_scales[:, g, :],
+                in_=w_grouped[:, g].rearrange("p n t -> p (n t)"),
+            )
+
+        x_grouped = [None] * CHUNKS
+        x_codes = [None] * CHUNKS
+        x_scales = [None] * CHUNKS
+        diff = [None] * CHUNKS
+
+        def transpose_chunk(c):
+            x_grouped[c] = work.tile([P, PASSES, CHUNK * P * PACK], BF16, name="x_grouped", align_bytes=64)
+            for g in range(PASSES):
+                xt = psum_t.tile([P, CHUNK, HALVES, P], F32)
+                for j in range(CHUNK):
+                    words = x_sb[c][:, j, g * K_PASS : (g + 1) * K_PASS].bitcast(F32)
+                    for u in range(HALVES):
+                        nc.tensor.transpose(xt[:, j, u, :], words[:, u * P : (u + 1) * P], ident[:])
+                nc.scalar.copy(
+                    out=x_grouped[c][:, g, :].bitcast(F32).rearrange("p (j r u) -> p j r u", j=CHUNK, u=HALVES),
+                    in_=xt[:].rearrange("p j u r -> p j r u"),
+                )
+
+        def quantise_chunk(c):
+            x_codes[c] = work.tile([P, PASSES, CHUNK * P], U32, name="x_codes", align_bytes=64)
+            x_scales[c] = work.tile([P, PASSES, CHUNK * P], U8, name="x_scales", align_bytes=64)
+            for g in range(PASSES):
+                nc.vector.quantize_mx(
+                    out=x_codes[c][:, g, :].bitcast(FP8X4),
+                    scales=x_scales[c][:, g, :],
+                    in_=x_grouped[c][:, g, :],
+                )
+
+        def difference(c):
+            by_tensor = psum_diff.tile([P, D], F32)
+            nc.tensor.matmul(out=by_tensor[:], lhsT=plus_one[:], rhs=cand[c][:, 0, :], start=True, stop=False)
+            nc.tensor.matmul(out=by_tensor[:], lhsT=minus_one[:], rhs=x_sb[c][:, 0, DM:K], start=False, stop=True)
+            by_vector = work.tile([P, D], F32)
+            nc.vector.tensor_tensor(out=by_vector[:], in0=cand[c][:, 1, :], in1=x_sb[c][:, 1, DM:K], op=ALU.subtract)
+            diff[c] = [by_tensor, by_vector]
+
+        def gate(c):
+            z = work.tile([P, CHUNK, D], F32, name="z")
+            for j in range(CHUNK):
+                rows = slice(j * P, (j + 1) * P)
+                acc = psum_acc.tile([P, D], F32)
+                for g in range(PASSES):
+                    nc.tensor.matmul_mx(
+                        out=acc[:],
+                        lhsT=x_codes[c][:, g, rows].bitcast(FP8X4),
+                        lhsT_scale=x_scales[c][:, g, rows],
+                        rhs=w_codes[:, g, :].bitcast(FP8X4),
+                        rhs_scale=w_scales[:, g, :],
+                        start=(g == 0),
+                        stop=(g == PASSES - 1),
+                    )
+                nc.scalar.activation(out=z[:, j, :], in_=acc[:], func=SIGMOID)
+            return z
+
+        def blend(c, z):
+            step = work.tile([P, CHUNK, D], F32, name="step")
+            result = work.tile([P, CHUNK, D], F32, name="result")
+            for j in range(CHUNK):
+                row_mask = mask_f32[:, c * CHUNK + j : c * CHUNK + j + 1]
+                nc.vector.scalar_tensor_tensor(
+                    out=step[:, j, :], in0=z[:, j, :], scalar=row_mask, in1=diff[c][j][:],
+                    op0=ALU.mult, op1=ALU.mult,
+                )
+            for j in range(CHUNK):
+                row_mask = mask_f32[:, c * CHUNK + j : c * CHUNK + j + 1]
+                nc.vector.scalar_tensor_tensor(
+                    out=result[:, j, :], in0=x_sb[c][:, j, DM:K], scalar=row_mask, in1=step[:, j, :],
+                    op0=ALU.mult, op1=ALU.add,
+                )
+                nc.sync.dma_start(out=out_rows[:, c * CHUNK + j, :], in_=result[:, j, :])
+
+        transpose_chunk(0)
+        quantise_chunk(0)
+        difference(0)
+        for c in range(CHUNKS):
+            if c + 1 < CHUNKS:
+                transpose_chunk(c + 1)
+            z = gate(c)
+            if c + 1 < CHUNKS:
+                quantise_chunk(c + 1)
+                difference(c + 1)
+            blend(c, z)

@@ -19,11 +19,14 @@ D = 512
 DM = 1024
 K = DM + D
 PASSES = K // K_PASS
+M_PASSES = DM // K_PASS
 ROW_TILES = ROWS // P
-CHUNK = 2
-CHUNKS = ROW_TILES // CHUNK
+CHUNK_SIZES = (1, 1, 2, 2, 2)
+CHUNKS = len(CHUNK_SIZES)
+STARTS = [sum(CHUNK_SIZES[:c]) for c in range(CHUNKS)]
 HALVES = 2
 VECTOR_COLS = D // 2
+TENSOR_DIFFS = (2, 4, 6, 7)
 
 FLOPS = 2 * ROWS * K * D
 
@@ -40,7 +43,8 @@ def tile_updatefunction_pb_kernel(tc, node_state, message, h_tilda, mask, w_z, u
     with ExitStack() as ctx:
         const = ctx.enter_context(tc.tile_pool(name="const", bufs=1))
         weights = ctx.enter_context(tc.tile_pool(name="weights", bufs=1))
-        work = ctx.enter_context(tc.tile_pool(name="work", bufs=CHUNKS))
+        rows_pool = ctx.enter_context(tc.tile_pool(name="rows_pool", bufs=1))
+        work = ctx.enter_context(tc.tile_pool(name="work", bufs=ROW_TILES))
         psum_t = ctx.enter_context(tc.psum_pool(name="psum_t", bufs=3))
         psum_acc = ctx.enter_context(tc.psum_pool(name="psum_acc", bufs=3))
         psum_diff = ctx.enter_context(tc.psum_pool(name="psum_diff", bufs=2))
@@ -61,83 +65,105 @@ def tile_updatefunction_pb_kernel(tc, node_state, message, h_tilda, mask, w_z, u
         nc.vector.tensor_copy(out=mask_f32[:], in_=mask_bf[:])
 
         w_raw = weights.tile([P, PASSES, PACK, D], BF16)
-        for g in range(PASSES):
-            w_pass = w_z[g * K_PASS : (g + 1) * K_PASS, :] if g < DM // K_PASS else u_z
+        x_sb = [rows_pool.tile([P, CHUNK_SIZES[c], K], BF16, name=f"x_sb{c}") for c in range(CHUNKS)]
+        cand = [rows_pool.tile([P, CHUNK_SIZES[c], D], BF16, name=f"cand{c}") for c in range(CHUNKS)]
+
+        def load_w(g):
+            w_pass = w_z[g * K_PASS : (g + 1) * K_PASS, :] if g < M_PASSES else u_z
             nc.sync.dma_start(
                 out=w_raw[:, g].rearrange("p (u e) n -> p u (e n)", u=HALVES),
                 in_=w_pass.rearrange("(u p e) n -> p u (e n)", u=HALVES, p=P),
             )
-        x_sb = []
-        cand = []
-        for c in range(CHUNKS):
-            tiles = slice(c * CHUNK, (c + 1) * CHUNK)
-            x_c = work.tile([P, CHUNK, K], BF16, name="x_sb")
-            nc.sync.dma_start(out=x_c[:, :, 0:DM], in_=m_rows[:, tiles, :])
-            nc.sync.dma_start(out=x_c[:, :, DM:K], in_=h_rows[:, tiles, :])
-            cand_c = work.tile([P, CHUNK, D], BF16, name="cand")
-            nc.sync.dma_start(out=cand_c[:], in_=cand_rows[:, tiles, :])
-            x_sb.append(x_c)
-            cand.append(cand_c)
+
+        def load_rows(dest, source, c):
+            nc.sync.dma_start(out=dest, in_=source[:, STARTS[c] : STARTS[c] + CHUNK_SIZES[c], :])
+
+        def load_m(c):
+            load_rows(x_sb[c][:, :, 0:DM], m_rows, c)
+
+        def load_h(c):
+            load_rows(x_sb[c][:, :, DM:K], h_rows, c)
+
+        def load_cand(c):
+            load_rows(cand[c][:], cand_rows, c)
+
+        load_w(0)
+        load_m(0)
+        load_w(1)
+        load_h(0)
+        load_w(2)
+        load_cand(0)
+        for c in range(1, CHUNKS):
+            load_m(c)
+            load_h(c)
+            load_cand(c)
 
         w_grouped = weights.tile([P, PASSES, D, PACK], BF16, align_bytes=64)
         w_codes = weights.tile([P, PASSES, D], U32, align_bytes=64)
         w_scales = weights.tile([P, PASSES, D], U8, align_bytes=64)
 
-        def regroup_w(copy, g, cols):
+        def regroup_cols(copy, g, cols):
             copy(
                 out=w_grouped[:, g, cols, :].rearrange("p (c i) t -> p c t i", i=4),
                 in_=w_raw[:, g, :, cols].rearrange("p t (c i) -> p c t i", i=4),
             )
 
-        for g in range(PASSES):
-            regroup_w(nc.vector.tensor_copy, g, slice(0, VECTOR_COLS))
-            regroup_w(nc.scalar.copy, g, slice(VECTOR_COLS, D))
-        for g in range(PASSES):
+        def regroup_w(g):
+            regroup_cols(nc.vector.tensor_copy, g, slice(0, VECTOR_COLS))
+            regroup_cols(nc.scalar.copy, g, slice(VECTOR_COLS, D))
+
+        def quantise_w(g):
             nc.vector.quantize_mx(
                 out=w_codes[:, g, :].bitcast(FP8X4),
                 scales=w_scales[:, g, :],
                 in_=w_grouped[:, g].rearrange("p n t -> p (n t)"),
             )
 
-        x_grouped = [None] * CHUNKS
-        x_codes = [None] * CHUNKS
-        x_scales = [None] * CHUNKS
-        diff = [None] * CHUNKS
+        x_grouped = [rows_pool.tile([P, PASSES, CHUNK_SIZES[c] * P * PACK], BF16, name=f"x_grouped{c}", align_bytes=64) for c in range(CHUNKS)]
+        x_codes = [rows_pool.tile([P, PASSES, CHUNK_SIZES[c] * P], U32, name=f"x_codes{c}", align_bytes=64) for c in range(CHUNKS)]
+        x_scales = [rows_pool.tile([P, PASSES, CHUNK_SIZES[c] * P], U8, name=f"x_scales{c}", align_bytes=64) for c in range(CHUNKS)]
+        diff = [None] * ROW_TILES
 
         def transpose_chunk(c):
-            x_grouped[c] = work.tile([P, PASSES, CHUNK * P * PACK], BF16, name="x_grouped", align_bytes=64)
-            for g in range(PASSES):
-                xt = psum_t.tile([P, CHUNK, HALVES, P], F32)
-                for j in range(CHUNK):
+            size = CHUNK_SIZES[c]
+            for first in range(0, PASSES, 2 // size):
+                passes = range(first, min(first + 2 // size, PASSES))
+                xt = psum_t.tile([P, 2, HALVES, P], F32)
+                pairs = [(g, j) for g in passes for j in range(size)]
+                for slot, (g, j) in enumerate(pairs):
                     words = x_sb[c][:, j, g * K_PASS : (g + 1) * K_PASS].bitcast(F32)
                     for u in range(HALVES):
-                        nc.tensor.transpose(xt[:, j, u, :], words[:, u * P : (u + 1) * P], ident[:])
+                        nc.tensor.transpose(xt[:, slot, u, :], words[:, u * P : (u + 1) * P], ident[:])
+                grouped = x_grouped[c][:, first : first + len(passes), :].rearrange("p g w -> p (g w)")
                 nc.scalar.copy(
-                    out=x_grouped[c][:, g, :].bitcast(F32).rearrange("p (j r u) -> p j r u", j=CHUNK, u=HALVES),
-                    in_=xt[:].rearrange("p j u r -> p j r u"),
+                    out=grouped.bitcast(F32).rearrange("p (s r u) -> p s r u", s=len(pairs), u=HALVES),
+                    in_=xt[:, 0 : len(pairs)].rearrange("p s u r -> p s r u"),
                 )
 
         def quantise_chunk(c):
-            x_codes[c] = work.tile([P, PASSES, CHUNK * P], U32, name="x_codes", align_bytes=64)
-            x_scales[c] = work.tile([P, PASSES, CHUNK * P], U8, name="x_scales", align_bytes=64)
-            for g in range(PASSES):
+            for passes in (slice(0, M_PASSES), slice(M_PASSES, PASSES)):
                 nc.vector.quantize_mx(
-                    out=x_codes[c][:, g, :].bitcast(FP8X4),
-                    scales=x_scales[c][:, g, :],
-                    in_=x_grouped[c][:, g, :],
+                    out=x_codes[c][:, passes, :].rearrange("p g w -> p (g w)").bitcast(FP8X4),
+                    scales=x_scales[c][:, passes, :].rearrange("p g w -> p (g w)"),
+                    in_=x_grouped[c][:, passes, :].rearrange("p g w -> p (g w)"),
                 )
 
         def difference(c):
-            by_tensor = psum_diff.tile([P, D], F32)
-            nc.tensor.matmul(out=by_tensor[:], lhsT=plus_one[:], rhs=cand[c][:, 0, :], start=True, stop=False)
-            nc.tensor.matmul(out=by_tensor[:], lhsT=minus_one[:], rhs=x_sb[c][:, 0, DM:K], start=False, stop=True)
-            by_vector = work.tile([P, D], F32)
-            nc.vector.tensor_tensor(out=by_vector[:], in0=cand[c][:, 1, :], in1=x_sb[c][:, 1, DM:K], op=ALU.subtract)
-            diff[c] = [by_tensor, by_vector]
+            for j in range(CHUNK_SIZES[c]):
+                i = STARTS[c] + j
+                if i in TENSOR_DIFFS:
+                    by_tensor = psum_diff.tile([P, D], F32)
+                    nc.tensor.matmul(out=by_tensor[:], lhsT=plus_one[:], rhs=cand[c][:, j, :], start=True, stop=False)
+                    nc.tensor.matmul(out=by_tensor[:], lhsT=minus_one[:], rhs=x_sb[c][:, j, DM:K], start=False, stop=True)
+                    diff[i] = by_tensor
+                else:
+                    by_vector = work.tile([P, D], F32)
+                    nc.vector.tensor_tensor(out=by_vector[:], in0=cand[c][:, j, :], in1=x_sb[c][:, j, DM:K], op=ALU.subtract)
+                    diff[i] = by_vector
 
         def gate(c):
-            z = work.tile([P, CHUNK, D], F32, name="z")
-            for j in range(CHUNK):
+            gates = []
+            for j in range(CHUNK_SIZES[c]):
                 rows = slice(j * P, (j + 1) * P)
                 acc = psum_acc.tile([P, D], F32)
                 for g in range(PASSES):
@@ -150,34 +176,42 @@ def tile_updatefunction_pb_kernel(tc, node_state, message, h_tilda, mask, w_z, u
                         start=(g == 0),
                         stop=(g == PASSES - 1),
                     )
-                nc.scalar.activation(out=z[:, j, :], in_=acc[:], func=SIGMOID)
-            return z
+                z = work.tile([P, D], F32)
+                nc.scalar.activation(out=z[:], in_=acc[:], func=SIGMOID)
+                gates.append(z)
+            return gates
 
-        def blend(c, z):
-            step = work.tile([P, CHUNK, D], F32, name="step")
-            result = work.tile([P, CHUNK, D], F32, name="result")
-            for j in range(CHUNK):
-                row_mask = mask_f32[:, c * CHUNK + j : c * CHUNK + j + 1]
+        def blend(c, gates):
+            steps = []
+            for j in range(CHUNK_SIZES[c]):
+                i = STARTS[c] + j
+                step = work.tile([P, D], F32)
                 nc.vector.scalar_tensor_tensor(
-                    out=step[:, j, :], in0=z[:, j, :], scalar=row_mask, in1=diff[c][j][:],
+                    out=step[:], in0=gates[j][:], scalar=mask_f32[:, i : i + 1], in1=diff[i][:],
                     op0=ALU.mult, op1=ALU.mult,
                 )
-            for j in range(CHUNK):
-                row_mask = mask_f32[:, c * CHUNK + j : c * CHUNK + j + 1]
+                steps.append(step)
+            for j in range(CHUNK_SIZES[c]):
+                i = STARTS[c] + j
+                result = work.tile([P, D], F32)
                 nc.vector.scalar_tensor_tensor(
-                    out=result[:, j, :], in0=x_sb[c][:, j, DM:K], scalar=row_mask, in1=step[:, j, :],
+                    out=result[:], in0=x_sb[c][:, j, DM:K], scalar=mask_f32[:, i : i + 1], in1=steps[j][:],
                     op0=ALU.mult, op1=ALU.add,
                 )
-                nc.sync.dma_start(out=out_rows[:, c * CHUNK + j, :], in_=result[:, j, :])
+                nc.sync.dma_start(out=out_rows[:, i, :], in_=result[:])
 
         transpose_chunk(0)
+        for g in range(PASSES):
+            regroup_w(g)
         quantise_chunk(0)
+        for g in range(PASSES):
+            quantise_w(g)
         difference(0)
         for c in range(CHUNKS):
             if c + 1 < CHUNKS:
                 transpose_chunk(c + 1)
-            z = gate(c)
+            gates = gate(c)
             if c + 1 < CHUNKS:
                 quantise_chunk(c + 1)
                 difference(c + 1)
-            blend(c, z)
+            blend(c, gates)

@@ -24,6 +24,8 @@ ROW_TILES = ROWS // P
 CHUNK_SIZES = (1, 1, 2, 2, 2)
 CHUNKS = len(CHUNK_SIZES)
 STARTS = [sum(CHUNK_SIZES[:c]) for c in range(CHUNKS)]
+PLACE = [(c, j) for c in range(CHUNKS) for j in range(CHUNK_SIZES[c])]
+ALL, M_PART, H_PART = slice(0, PASSES), slice(0, M_PASSES), slice(M_PASSES, PASSES)
 HALVES = 2
 VECTOR_COLS = D // 2
 TENSOR_DIFFS = (2, 4, 6, 7)
@@ -55,6 +57,8 @@ def tile_updatefunction_pb_kernel(tc, node_state, message, h_tilda, mask, w_z, u
         nc.vector.memset(zero[:], 0.0)
         warm = const.tile([P, 1], F32)
         nc.scalar.activation(out=warm[:], in_=zero[:], func=SIGMOID)
+        ctx.enter_context(tc.manual_schedule())
+
         ident = const.tile([P, P], F32)
         make_identity(nc, ident[:])
         plus_one = const.tile([P, P], BF16)
@@ -62,7 +66,6 @@ def tile_updatefunction_pb_kernel(tc, node_state, message, h_tilda, mask, w_z, u
         minus_one = const.tile([P, P], BF16)
         nc.vector.tensor_scalar_mul(out=minus_one[:], in0=ident[:], scalar1=-1.0)
         mask_f32 = const.tile([P, ROW_TILES], F32)
-        nc.vector.tensor_copy(out=mask_f32[:], in_=mask_bf[:])
 
         w_raw = weights.tile([P, PASSES, PACK, D], BF16)
         x_sb = [rows_pool.tile([P, CHUNK_SIZES[c], K], BF16, name=f"x_sb{c}") for c in range(CHUNKS)]
@@ -123,10 +126,12 @@ def tile_updatefunction_pb_kernel(tc, node_state, message, h_tilda, mask, w_z, u
         x_codes = [rows_pool.tile([P, PASSES, CHUNK_SIZES[c] * P], U32, name=f"x_codes{c}", align_bytes=64) for c in range(CHUNKS)]
         x_scales = [rows_pool.tile([P, PASSES, CHUNK_SIZES[c] * P], U8, name=f"x_scales{c}", align_bytes=64) for c in range(CHUNKS)]
         diff = [None] * ROW_TILES
+        gates = [None] * ROW_TILES
+        steps = [None] * ROW_TILES
 
-        def transpose_chunk(c):
+        def transpose(c, of_passes):
             size = CHUNK_SIZES[c]
-            for first in range(0, PASSES, 2 // size):
+            for first in range(of_passes.start, of_passes.stop, 2 // size):
                 passes = range(first, min(first + 2 // size, PASSES))
                 xt = psum_t.tile([P, 2, HALVES, P], F32)
                 pairs = [(g, j) for g in passes for j in range(size)]
@@ -140,29 +145,26 @@ def tile_updatefunction_pb_kernel(tc, node_state, message, h_tilda, mask, w_z, u
                     in_=xt[:, 0 : len(pairs)].rearrange("p s u r -> p s r u"),
                 )
 
-        def quantise_chunk(c):
-            for passes in (slice(0, M_PASSES), slice(M_PASSES, PASSES)):
-                nc.vector.quantize_mx(
-                    out=x_codes[c][:, passes, :].rearrange("p g w -> p (g w)").bitcast(FP8X4),
-                    scales=x_scales[c][:, passes, :].rearrange("p g w -> p (g w)"),
-                    in_=x_grouped[c][:, passes, :].rearrange("p g w -> p (g w)"),
-                )
+        def quantise(c, passes):
+            nc.vector.quantize_mx(
+                out=x_codes[c][:, passes, :].rearrange("p g w -> p (g w)").bitcast(FP8X4),
+                scales=x_scales[c][:, passes, :].rearrange("p g w -> p (g w)"),
+                in_=x_grouped[c][:, passes, :].rearrange("p g w -> p (g w)"),
+            )
 
-        def difference(c):
-            for j in range(CHUNK_SIZES[c]):
-                i = STARTS[c] + j
-                if i in TENSOR_DIFFS:
-                    by_tensor = psum_diff.tile([P, D], F32)
-                    nc.tensor.matmul(out=by_tensor[:], lhsT=plus_one[:], rhs=cand[c][:, j, :], start=True, stop=False)
-                    nc.tensor.matmul(out=by_tensor[:], lhsT=minus_one[:], rhs=x_sb[c][:, j, DM:K], start=False, stop=True)
-                    diff[i] = by_tensor
-                else:
-                    by_vector = work.tile([P, D], F32)
-                    nc.vector.tensor_tensor(out=by_vector[:], in0=cand[c][:, j, :], in1=x_sb[c][:, j, DM:K], op=ALU.subtract)
-                    diff[i] = by_vector
+        def difference(i):
+            c, j = PLACE[i]
+            if i in TENSOR_DIFFS:
+                by_tensor = psum_diff.tile([P, D], F32)
+                nc.tensor.matmul(out=by_tensor[:], lhsT=plus_one[:], rhs=cand[c][:, j, :], start=True, stop=False)
+                nc.tensor.matmul(out=by_tensor[:], lhsT=minus_one[:], rhs=x_sb[c][:, j, DM:K], start=False, stop=True)
+                diff[i] = by_tensor
+            else:
+                by_vector = work.tile([P, D], F32)
+                nc.vector.tensor_tensor(out=by_vector[:], in0=cand[c][:, j, :], in1=x_sb[c][:, j, DM:K], op=ALU.subtract)
+                diff[i] = by_vector
 
         def gate(c):
-            gates = []
             for j in range(CHUNK_SIZES[c]):
                 rows = slice(j * P, (j + 1) * P)
                 acc = psum_acc.tile([P, D], F32)
@@ -178,40 +180,67 @@ def tile_updatefunction_pb_kernel(tc, node_state, message, h_tilda, mask, w_z, u
                     )
                 z = work.tile([P, D], F32)
                 nc.scalar.activation(out=z[:], in_=acc[:], func=SIGMOID)
-                gates.append(z)
-            return gates
+                gates[STARTS[c] + j] = z
 
-        def blend(c, gates):
-            steps = []
-            for j in range(CHUNK_SIZES[c]):
-                i = STARTS[c] + j
-                step = work.tile([P, D], F32)
-                nc.vector.scalar_tensor_tensor(
-                    out=step[:], in0=gates[j][:], scalar=mask_f32[:, i : i + 1], in1=diff[i][:],
-                    op0=ALU.mult, op1=ALU.mult,
-                )
-                steps.append(step)
-            for j in range(CHUNK_SIZES[c]):
-                i = STARTS[c] + j
-                result = work.tile([P, D], F32)
-                nc.vector.scalar_tensor_tensor(
-                    out=result[:], in0=x_sb[c][:, j, DM:K], scalar=mask_f32[:, i : i + 1], in1=steps[j][:],
-                    op0=ALU.mult, op1=ALU.add,
-                )
-                nc.sync.dma_start(out=out_rows[:, i, :], in_=result[:])
+        def blend_step(i):
+            step = work.tile([P, D], F32)
+            nc.vector.scalar_tensor_tensor(
+                out=step[:], in0=gates[i][:], scalar=mask_f32[:, i : i + 1], in1=diff[i][:],
+                op0=ALU.mult, op1=ALU.mult,
+            )
+            steps[i] = step
 
-        transpose_chunk(0)
-        for g in range(PASSES):
-            regroup_w(g)
-        quantise_chunk(0)
-        for g in range(PASSES):
-            quantise_w(g)
+        def blend_result(i):
+            c, j = PLACE[i]
+            result = work.tile([P, D], F32)
+            nc.vector.scalar_tensor_tensor(
+                out=result[:], in0=x_sb[c][:, j, DM:K], scalar=mask_f32[:, i : i + 1], in1=steps[i][:],
+                op0=ALU.mult, op1=ALU.add,
+            )
+            nc.sync.dma_start(out=out_rows[:, i, :], in_=result[:])
+
+        def tiles_of(c):
+            return range(STARTS[c], STARTS[c] + CHUNK_SIZES[c])
+
+        regroup_w(0)
+        transpose(0, M_PART)
+        quantise_w(0)
+        regroup_w(1)
+        transpose(0, H_PART)
+        quantise(0, M_PART)
+        regroup_w(2)
+        quantise(0, H_PART)
+        quantise_w(1)
         difference(0)
-        for c in range(CHUNKS):
+        nc.vector.tensor_copy(out=mask_f32[:], in_=mask_bf[:])
+        quantise_w(2)
+        transpose(1, ALL)
+        gate(0)
+        quantise(1, M_PART)
+        quantise(1, H_PART)
+        difference(1)
+        transpose(2, ALL)
+        gate(1)
+        for i in tiles_of(2):
+            difference(i)
+        blend_step(0)
+        quantise(2, M_PART)
+        quantise(2, H_PART)
+        blend_result(0)
+        for c in range(2, CHUNKS):
             if c + 1 < CHUNKS:
-                transpose_chunk(c + 1)
-            gates = gate(c)
+                transpose(c + 1, ALL)
+            gate(c)
+            for i in tiles_of(c - 1):
+                blend_step(i)
             if c + 1 < CHUNKS:
-                quantise_chunk(c + 1)
-                difference(c + 1)
-            blend(c, gates)
+                quantise(c + 1, M_PART)
+                quantise(c + 1, H_PART)
+                for i in tiles_of(c + 1):
+                    difference(i)
+            for i in tiles_of(c - 1):
+                blend_result(i)
+        for i in tiles_of(CHUNKS - 1):
+            blend_step(i)
+        for i in tiles_of(CHUNKS - 1):
+            blend_result(i)

@@ -222,7 +222,8 @@ def tile_updatefunction_pb_kernel(tc, node_state, message, h_tilda, mask, w_z, u
         transpose(2, ALL)
         gate(1)
         for i in tiles_of(2):
-            difference(i)
+            if i not in TENSOR_DIFFS:
+                difference(i)
         blend_step(0)
         quantise(2, M_PART)
         quantise(2, H_PART)
@@ -231,13 +232,17 @@ def tile_updatefunction_pb_kernel(tc, node_state, message, h_tilda, mask, w_z, u
             if c + 1 < CHUNKS:
                 transpose(c + 1, ALL)
             gate(c)
+            for i in tiles_of(c):
+                if i in TENSOR_DIFFS:
+                    difference(i)
             for i in tiles_of(c - 1):
                 blend_step(i)
             if c + 1 < CHUNKS:
                 quantise(c + 1, M_PART)
                 quantise(c + 1, H_PART)
                 for i in tiles_of(c + 1):
-                    difference(i)
+                    if i not in TENSOR_DIFFS:
+                        difference(i)
             for i in tiles_of(c - 1):
                 blend_result(i)
         for i in tiles_of(CHUNKS - 1):

@@ -28,7 +28,7 @@ PLACE = [(c, j) for c in range(CHUNKS) for j in range(CHUNK_SIZES[c])]
 ALL, M_PART, H_PART = slice(0, PASSES), slice(0, M_PASSES), slice(M_PASSES, PASSES)
 HALVES = 2
 VECTOR_COLS = D // 2
-TENSOR_DIFFS = (2, 4, 6, 7)
+TENSOR_DIFFS = (4, 5, 6, 7)
 
 FLOPS = 2 * ROWS * K * D
 
@@ -193,11 +193,14 @@ def tile_updatefunction_pb_kernel(tc, node_state, message, h_tilda, mask, w_z, u
         def blend_result(i):
             c, j = PLACE[i]
             result = work.tile([P, D], F32)
-            nc.vector.scalar_tensor_tensor(
-                out=result[:], in0=x_sb[c][:, j, DM:K], scalar=mask_f32[:, i : i + 1], in1=steps[i][:],
-                op0=ALU.mult, op1=ALU.add,
-            )
-            nc.sync.dma_start(out=out_rows[:, i, :], in_=result[:])
+            parts = 2 if i == ROW_TILES - 1 else 1
+            for part in range(parts):
+                cols = slice(part * D // parts, (part + 1) * D // parts)
+                nc.vector.scalar_tensor_tensor(
+                    out=result[:, cols], in0=x_sb[c][:, j, DM + cols.start : DM + cols.stop],
+                    scalar=mask_f32[:, i : i + 1], in1=steps[i][:, cols], op0=ALU.mult, op1=ALU.add,
+                )
+                nc.sync.dma_start(out=out_rows[:, i, cols], in_=result[:, cols])
 
         def tiles_of(c):
             return range(STARTS[c], STARTS[c] + CHUNK_SIZES[c])

@@ -95,8 +95,11 @@ def tile_updatefunction_pb_kernel(tc, node_state, message, h_tilda, mask, w_z, u
         load_w(1)
         load_h(0)
         load_w(2)
+        load_m(1)
         load_cand(0)
-        for c in range(1, CHUNKS):
+        load_h(1)
+        load_cand(1)
+        for c in range(2, CHUNKS):
             load_m(c)
             load_h(c)
             load_cand(c)

@@ -27,7 +27,7 @@ STARTS = [sum(CHUNK_SIZES[:c]) for c in range(CHUNKS)]
 PLACE = [(c, j) for c in range(CHUNKS) for j in range(CHUNK_SIZES[c])]
 ALL, M_PART, H_PART = slice(0, PASSES), slice(0, M_PASSES), slice(M_PASSES, PASSES)
 HALVES = 2
-VECTOR_COLS = D // 2
+VECTOR_COLS = 5 * D // 8
 TENSOR_DIFFS = (4, 5, 6, 7)
 
 FLOPS = 2 * ROWS * K * D

from contextlib import ExitStack

import concourse.mybir as mybir
from concourse.masks import make_identity

F32 = mybir.dt.float32
BF16 = mybir.dt.bfloat16
U32 = mybir.dt.uint32
U8 = mybir.dt.uint8
FP8X4 = mybir.dt.float8_e4m3fn_x4
ALU = mybir.AluOpType
SIGMOID = mybir.ActivationFunctionType.Sigmoid

P = 128
PACK = 4
K_PASS = P * PACK
ROWS = 1024
D = 512
DM = 1024
K = DM + D
PASSES = K // K_PASS
M_PASSES = DM // K_PASS
ROW_TILES = ROWS // P
CHUNK_SIZES = (1, 1, 2, 2, 2)
CHUNKS = len(CHUNK_SIZES)
STARTS = [sum(CHUNK_SIZES[:c]) for c in range(CHUNKS)]
PLACE = [(c, j) for c in range(CHUNKS) for j in range(CHUNK_SIZES[c])]
ALL, M_PART, H_PART = slice(0, PASSES), slice(0, M_PASSES), slice(M_PASSES, PASSES)
HALVES = 2
VECTOR_COLS = 5 * D // 8
TENSOR_DIFFS = (4, 5, 6, 7)

FLOPS = 2 * ROWS * K * D


def tile_updatefunction_pb_kernel(tc, node_state, message, h_tilda, mask, w_z, u_z, out):
    nc = tc.nc

    h_rows = node_state.flatten_outer_dims().rearrange("(p i) d -> p i d", i=ROW_TILES)
    m_rows = message.flatten_outer_dims().rearrange("(p i) d -> p i d", i=ROW_TILES)
    cand_rows = h_tilda.rearrange("(p i) d -> p i d", i=ROW_TILES)
    mask_rows = mask.rearrange("b (q i) -> (b q) i", i=ROW_TILES)
    out_rows = out.flatten_outer_dims().rearrange("(p i) d -> p i d", i=ROW_TILES)

    with ExitStack() as ctx:
        const = ctx.enter_context(tc.tile_pool(name="const", bufs=1))
        weights = ctx.enter_context(tc.tile_pool(name="weights", bufs=1))
        rows_pool = ctx.enter_context(tc.tile_pool(name="rows_pool", bufs=1))
        work = ctx.enter_context(tc.tile_pool(name="work", bufs=ROW_TILES))
        psum_t = ctx.enter_context(tc.psum_pool(name="psum_t", bufs=3))
        psum_acc = ctx.enter_context(tc.psum_pool(name="psum_acc", bufs=3))
        psum_diff = ctx.enter_context(tc.psum_pool(name="psum_diff", bufs=2))

        mask_bf = const.tile([P, ROW_TILES], BF16)
        nc.scalar.dma_start(out=mask_bf[:], in_=mask_rows)
        zero = const.tile([P, 1], F32)
        nc.vector.memset(zero[:], 0.0)
        warm = const.tile([P, 1], F32)
        nc.scalar.activation(out=warm[:], in_=zero[:], func=SIGMOID)
        ctx.enter_context(tc.manual_schedule())

        ident = const.tile([P, P], F32)
        make_identity(nc, ident[:])
        plus_one = const.tile([P, P], BF16)
        nc.vector.tensor_copy(out=plus_one[:], in_=ident[:])
        minus_one = const.tile([P, P], BF16)
        nc.vector.tensor_scalar_mul(out=minus_one[:], in0=ident[:], scalar1=-1.0)
        mask_f32 = const.tile([P, ROW_TILES], F32)

        w_raw = weights.tile([P, PASSES, PACK, D], BF16)
        x_sb = [rows_pool.tile([P, CHUNK_SIZES[c], K], BF16, name=f"x_sb{c}") for c in range(CHUNKS)]
        cand = [rows_pool.tile([P, CHUNK_SIZES[c], D], BF16, name=f"cand{c}") for c in range(CHUNKS)]

        def load_w(g):
            w_pass = w_z[g * K_PASS : (g + 1) * K_PASS, :] if g < M_PASSES else u_z
            nc.sync.dma_start(
                out=w_raw[:, g].rearrange("p (u e) n -> p u (e n)", u=HALVES),
                in_=w_pass.rearrange("(u p e) n -> p u (e n)", u=HALVES, p=P),
            )

        def load_rows(dest, source, c):
            nc.sync.dma_start(out=dest, in_=source[:, STARTS[c] : STARTS[c] + CHUNK_SIZES[c], :])

        def load_m(c):
            load_rows(x_sb[c][:, :, 0:DM], m_rows, c)

        def load_h(c):
            load_rows(x_sb[c][:, :, DM:K], h_rows, c)

        def load_cand(c):
            load_rows(cand[c][:], cand_rows, c)

        load_w(0)
        load_m(0)
        load_w(1)
        load_h(0)
        load_w(2)
        load_m(1)
        load_cand(0)
        load_h(1)
        load_cand(1)
        for c in range(2, CHUNKS):
            load_m(c)
            load_h(c)
            load_cand(c)

        w_grouped = weights.tile([P, PASSES, D, PACK], BF16, align_bytes=64)
        w_codes = weights.tile([P, PASSES, D], U32, align_bytes=64)
        w_scales = weights.tile([P, PASSES, D], U8, align_bytes=64)

        def regroup_cols(copy, g, cols):
            copy(
                out=w_grouped[:, g, cols, :].rearrange("p (c i) t -> p c t i", i=4),
                in_=w_raw[:, g, :, cols].rearrange("p t (c i) -> p c t i", i=4),
            )

        def regroup_w(g):
            regroup_cols(nc.vector.tensor_copy, g, slice(0, VECTOR_COLS))
            regroup_cols(nc.scalar.copy, g, slice(VECTOR_COLS, D))

        def quantise_w(g):
            nc.vector.quantize_mx(
                out=w_codes[:, g, :].bitcast(FP8X4),
                scales=w_scales[:, g, :],
                in_=w_grouped[:, g].rearrange("p n t -> p (n t)"),
            )

        x_grouped = [rows_pool.tile([P, PASSES, CHUNK_SIZES[c] * P * PACK], BF16, name=f"x_grouped{c}", align_bytes=64) for c in range(CHUNKS)]
        x_codes = [rows_pool.tile([P, PASSES, CHUNK_SIZES[c] * P], U32, name=f"x_codes{c}", align_bytes=64) for c in range(CHUNKS)]
        x_scales = [rows_pool.tile([P, PASSES, CHUNK_SIZES[c] * P], U8, name=f"x_scales{c}", align_bytes=64) for c in range(CHUNKS)]
        diff = [None] * ROW_TILES
        gates = [None] * ROW_TILES
        steps = [None] * ROW_TILES

        def transpose(c, of_passes):
            size = CHUNK_SIZES[c]
            for first in range(of_passes.start, of_passes.stop, 2 // size):
                passes = range(first, min(first + 2 // size, PASSES))
                xt = psum_t.tile([P, 2, HALVES, P], F32)
                pairs = [(g, j) for g in passes for j in range(size)]
                for slot, (g, j) in enumerate(pairs):
                    words = x_sb[c][:, j, g * K_PASS : (g + 1) * K_PASS].bitcast(F32)
                    for u in range(HALVES):
                        nc.tensor.transpose(xt[:, slot, u, :], words[:, u * P : (u + 1) * P], ident[:])
                grouped = x_grouped[c][:, first : first + len(passes), :].rearrange("p g w -> p (g w)")
                nc.scalar.copy(
                    out=grouped.bitcast(F32).rearrange("p (s r u) -> p s r u", s=len(pairs), u=HALVES),
                    in_=xt[:, 0 : len(pairs)].rearrange("p s u r -> p s r u"),
                )

        def quantise(c, passes):
            nc.vector.quantize_mx(
                out=x_codes[c][:, passes, :].rearrange("p g w -> p (g w)").bitcast(FP8X4),
                scales=x_scales[c][:, passes, :].rearrange("p g w -> p (g w)"),
                in_=x_grouped[c][:, passes, :].rearrange("p g w -> p (g w)"),
            )

        def difference(i):
            c, j = PLACE[i]
            if i in TENSOR_DIFFS:
                by_tensor = psum_diff.tile([P, D], F32)
                nc.tensor.matmul(out=by_tensor[:], lhsT=plus_one[:], rhs=cand[c][:, j, :], start=True, stop=False)
                nc.tensor.matmul(out=by_tensor[:], lhsT=minus_one[:], rhs=x_sb[c][:, j, DM:K], start=False, stop=True)
                diff[i] = by_tensor
            else:
                by_vector = work.tile([P, D], F32)
                nc.vector.tensor_tensor(out=by_vector[:], in0=cand[c][:, j, :], in1=x_sb[c][:, j, DM:K], op=ALU.subtract)
                diff[i] = by_vector

        def gate(c):
            for j in range(CHUNK_SIZES[c]):
                rows = slice(j * P, (j + 1) * P)
                acc = psum_acc.tile([P, D], F32)
                for g in range(PASSES):
                    nc.tensor.matmul_mx(
                        out=acc[:],
                        lhsT=x_codes[c][:, g, rows].bitcast(FP8X4),
                        lhsT_scale=x_scales[c][:, g, rows],
                        rhs=w_codes[:, g, :].bitcast(FP8X4),
                        rhs_scale=w_scales[:, g, :],
                        start=(g == 0),
                        stop=(g == PASSES - 1),
                    )
                z = work.tile([P, D], F32)
                nc.scalar.activation(out=z[:], in_=acc[:], func=SIGMOID)
                gates[STARTS[c] + j] = z

        def blend_step(i):
            step = work.tile([P, D], F32)
            nc.vector.scalar_tensor_tensor(
                out=step[:], in0=gates[i][:], scalar=mask_f32[:, i : i + 1], in1=diff[i][:],
                op0=ALU.mult, op1=ALU.mult,
            )
            steps[i] = step

        def blend_result(i):
            c, j = PLACE[i]
            result = work.tile([P, D], F32)
            parts = 2 if i == ROW_TILES - 1 else 1
            for part in range(parts):
                cols = slice(part * D // parts, (part + 1) * D // parts)
                nc.vector.scalar_tensor_tensor(
                    out=result[:, cols], in0=x_sb[c][:, j, DM + cols.start : DM + cols.stop],
                    scalar=mask_f32[:, i : i + 1], in1=steps[i][:, cols], op0=ALU.mult, op1=ALU.add,
                )
                nc.sync.dma_start(out=out_rows[:, i, cols], in_=result[:, cols])

        def tiles_of(c):
            return range(STARTS[c], STARTS[c] + CHUNK_SIZES[c])

        regroup_w(0)
        transpose(0, M_PART)
        quantise_w(0)
        regroup_w(1)
        transpose(0, H_PART)
        quantise(0, M_PART)
        regroup_w(2)
        quantise(0, H_PART)
        quantise_w(1)
        difference(0)
        nc.vector.tensor_copy(out=mask_f32[:], in_=mask_bf[:])
        quantise_w(2)
        transpose(1, ALL)
        gate(0)
        quantise(1, M_PART)
        quantise(1, H_PART)
        difference(1)
        transpose(2, ALL)
        gate(1)
        for i in tiles_of(2):
            if i not in TENSOR_DIFFS:
                difference(i)
        blend_step(0)
        quantise(2, M_PART)
        quantise(2, H_PART)
        blend_result(0)
        for c in range(2, CHUNKS):
            if c + 1 < CHUNKS:
                transpose(c + 1, ALL)
            gate(c)
            for i in tiles_of(c):
                if i in TENSOR_DIFFS:
                    difference(i)
            for i in tiles_of(c - 1):
                blend_step(i)
            if c + 1 < CHUNKS:
                quantise(c + 1, M_PART)
                quantise(c + 1, H_PART)
                for i in tiles_of(c + 1):
                    if i not in TENSOR_DIFFS:
                        difference(i)
            for i in tiles_of(c - 1):
                blend_result(i)
        for i in tiles_of(CHUNKS - 1):
            blend_step(i)
        for i in tiles_of(CHUNKS - 1):
            blend_result(i)
